import numpy as np
import ml_dtypes


def mxq(x, axis, fmt="e4m3"):
    dtype, down = {"e4m3": (ml_dtypes.float8_e4m3fn, 7), "e5m2": (ml_dtypes.float8_e5m2, 14)}[fmt]
    v = np.moveaxis(np.asarray(x, np.float32).astype(ml_dtypes.bfloat16).astype(np.float64), axis, -1)
    blocks = v.reshape(v.shape[:-1] + (-1, 32))
    amax = np.abs(blocks).max(-1, keepdims=True)
    byte = np.maximum(np.where(amax > 0, np.frexp(amax)[1] - 1 + 127, 0) - down, 1)
    scale = np.exp2(byte - 127.0)
    codes = (blocks / scale).astype(np.float32).astype(dtype).astype(np.float64)
    return np.moveaxis((codes * scale).reshape(v.shape), -1, axis)


WIDE = False


def mx_kscale(k):
    if not WIDE:
        return np.ones(k)
    levels = np.array([10, -10, 5, -5, 0])
    if k % 512:
        return np.exp2(np.random.permutation(np.resize(levels, k // 32))).repeat(32)
    a = np.empty((k // 512, 16))
    for p in range(k // 512):
        a[p, :8] = np.random.permutation(np.resize(levels, 8))
        for g in range(8):
            far = levels[np.abs(levels - a[p, g]) >= 10]
            a[p, g + 8] = far[np.random.randint(len(far))]
    return np.exp2(a.ravel()).repeat(32)


BF16 = ml_dtypes.bfloat16


def bf(x):
    return np.asarray(x, np.float32).astype(BF16)


def f64(x):
    return np.asarray(x).astype(np.float64)


B, S, DIM, H, NOPE, ROPE, VHD, KV_RANK = 2, 256, 2048, 16, 128, 64, 128, 512
QKHD = NOPE + ROPE
HALF = ROPE // 2


def rope(u, cos, sin):
    ur = u.reshape(u.shape[:-1] + (HALF, 2))
    a, b = ur[..., 0], ur[..., 1]
    c = cos[None, :, None, :]
    s = sin[None, :, None, :]
    return np.stack([a * c - b * s, a * s + b * c], axis=-1).reshape(u.shape)


def setup_inputs():
    s = mx_kscale(DIM)
    inv_freq = 1.0 / 10000.0 ** (np.arange(0, ROPE, 2) / ROPE)
    ang = np.arange(S)[:, None] * inv_freq[None, :]
    return {"x": bf(np.random.standard_normal((B, S, DIM)) * s),
            "wq_w": bf(np.random.standard_normal((DIM, H * QKHD)) / np.sqrt(DIM) / s[:, None]),
            "wq_b": bf(np.random.standard_normal(H * QKHD) * 0.2),
            "cos": bf(np.cos(ang)), "sin": bf(np.sin(ang))}


def reference(x, wq_w, wq_b, cos, sin):
    q = (mxq(f64(x), 2, "e4m3") @ mxq(f64(wq_w), 0, "e4m3")) + f64(wq_b)
    q = q.reshape(B, S, H, QKHD)
    return np.concatenate([q[..., :NOPE], rope(q[..., NOPE:], f64(cos), f64(sin))], axis=-1)

@@ -1,0 +1,295 @@
+from contextlib import ExitStack
+
+import concourse.mybir as mybir
+from concourse.masks import make_identity
+
+F32 = mybir.dt.float32
+BF16 = mybir.dt.bfloat16
+U32 = mybir.dt.uint32
+U8 = mybir.dt.uint8
+FP8X4 = mybir.dt.float8_e4m3fn_x4
+ADD = mybir.AluOpType.add
+MULT = mybir.AluOpType.mult
+
+P = 128
+PACK = 4
+K_PASS = P * PACK
+TOKENS = 512
+DIM = 2048
+HEAD = 192
+NOPE = 128
+ROPE = 64
+PAIRS = ROPE // 2
+COLS = 16 * HEAD
+BANK = 512
+PSUM_BANKS = 8
+
+TOKEN_TILES = TOKENS // P
+PASSES = DIM // K_PASS
+PANELS = COLS // BANK
+UNITS = PANELS * PASSES
+
+MAX_HEADS = 3
+Q_WIDTH = BANK + NOPE
+
+PANELS_AHEAD = 4
+GROUPED_AHEAD = 4
+CODES_AHEAD = 6
+RESULT_TILES = 3
+
+GPSIMD_COLUMNS = 320
+RUN = 4
+
+FLOPS = 2 * TOKENS * DIM * COLS
+
+
+def first_column(n):
+    return (PANELS - 1 - n) * BANK
+
+
+def tile_mla_pb_kernel(tc, x, wq_w, wq_b, cos, sin, out):
+    nc = tc.nc
+    x_rows = x.flatten_outer_dims()
+    out_rows = out.rearrange("b s h d -> (b s) (h d)")
+
+    with ExitStack() as stack:
+        const = stack.enter_context(tc.tile_pool(name="const", bufs=1))
+        x_pool = stack.enter_context(tc.tile_pool(name="x_pool", bufs=TOKEN_TILES))
+        raw_pool = stack.enter_context(tc.tile_pool(name="raw_pool", bufs=PANELS_AHEAD * PASSES))
+        grouped_pool = stack.enter_context(tc.tile_pool(name="grouped_pool", bufs=GROUPED_AHEAD))
+        first_pool = stack.enter_context(tc.tile_pool(name="first_pool", bufs=1))
+        codes_pool = stack.enter_context(tc.tile_pool(name="codes_pool", bufs=CODES_AHEAD))
+        q_pool = stack.enter_context(tc.tile_pool(name="q_pool", bufs=RESULT_TILES))
+        psum = stack.enter_context(tc.psum_pool(name="psum", bufs=PSUM_BANKS))
+
+        identity = const.tile([P, P], F32, name="identity")
+        make_identity(nc, identity[:])
+        identity_bf = const.tile([P, P], BF16, name="identity_bf")
+        make_identity(nc, identity_bf[:])
+
+        stack.enter_context(tc.manual_schedule())
+
+        w_raw = {}
+
+        def load_panel(n):
+            for g in range(PASSES):
+                w_tile = raw_pool.tile([P, PACK, BANK], BF16, name="w_raw")
+                nc.sync.dma_start(
+                    out=w_tile[:],
+                    in_=wq_w[
+                        g * K_PASS : (g + 1) * K_PASS, first_column(n) : first_column(n) + BANK
+                    ].rearrange("(p j) c -> p j c", j=PACK),
+                )
+                w_raw[n * PASSES + g] = w_tile
+
+        bias_rows = const.tile([P, BANK], BF16, name="bias_rows")
+        nc.vector.memset(bias_rows[:].bitcast(F32), 0.0)
+        nc.sync.dma_start(out=bias_rows[0:PANELS, :], in_=wq_b.rearrange("(c w) -> c w", w=BANK))
+        cos_sb = const.tile([P, 2, PAIRS], BF16, name="cos_sb")
+        sin_sb = const.tile([P, 2, PAIRS], BF16, name="sin_sb")
+        nc.scalar.dma_start(out=cos_sb[:], in_=cos.rearrange("(a p) j -> p a j", p=P))
+        nc.scalar.dma_start(out=sin_sb[:], in_=sin.rearrange("(a p) j -> p a j", p=P))
+
+        x_raw = []
+        for t in range(TOKEN_TILES):
+            x_tile = x_pool.tile([P, DIM], BF16, name="x_raw")
+            nc.sync.dma_start(out=x_tile[:], in_=x_rows[t * P : (t + 1) * P, :])
+            x_raw.append(x_tile)
+
+        for n in range(PANELS_AHEAD):
+            load_panel(n)
+
+        bias_sb = const.tile([P, COLS], F32, name="bias_sb")
+
+        def spread_bias(c):
+            spread = psum.tile([P, BANK], F32, name="spread", tag="bank")
+            nc.tensor.matmul(
+                out=spread[:],
+                lhsT=identity_bf[:, c : c + 1].to_broadcast([P, P]),
+                rhs=bias_rows[:],
+                start=True,
+                stop=True,
+            )
+            nc.vector.tensor_copy(out=bias_sb[:, c * BANK : (c + 1) * BANK], in_=spread[:])
+
+        x_grouped = []
+        x_codes = []
+        x_scales = []
+
+        def x_flip(t):
+            words = x_raw[t][:].bitcast(F32)
+            grouped = x_pool.tile([P, PASSES * P * PACK], BF16, name="x_grouped", align_bytes=64)
+            grouped_words = grouped[:].bitcast(F32).rearrange(
+                "p (g r u) -> p g r u", g=PASSES, u=2
+            )
+            for half in range(2):
+                flipped = psum.tile([P, 2, 2, P], F32, name="flipped", tag="bank")
+                for gg in range(2):
+                    for u in range(2):
+                        first_word = (2 * half + gg) * 2 * P
+                        nc.tensor.transpose(
+                            flipped[:, gg, u, :],
+                            words[:, first_word + u : first_word + 2 * P : 2],
+                            identity[:],
+                        )
+                nc.scalar.copy(
+                    out=grouped_words[:, 2 * half : 2 * half + 2],
+                    in_=flipped[:].rearrange("p g u r -> p g r u"),
+                )
+            x_grouped.append(grouped)
+
+        def x_quantise(t):
+            codes = x_pool.tile([P, PASSES * P], U32, name="x_codes", align_bytes=64)
+            scales = x_pool.tile([P, PASSES * P], U8, name="x_scales", align_bytes=64)
+            nc.vector.quantize_mx(
+                out=codes[:].bitcast(FP8X4), scales=scales[:], in_=x_grouped[t][:]
+            )
+            x_codes.append(codes)
+            x_scales.append(scales)
+
+        for t in range(TOKEN_TILES):
+            for c in range(2 * t, min(2 * t + 2, PANELS)):
+                spread_bias(c)
+            x_flip(t)
+            x_quantise(t)
+
+        cos_table = const.tile([P, 2, MAX_HEADS, PAIRS, 2], BF16, name="cos_table")
+        sin_table = const.tile([P, 2, 2, MAX_HEADS, PAIRS], BF16, name="sin_table")
+        nc.vector.tensor_copy(
+            out=cos_table[:],
+            in_=cos_sb[:].unsqueeze(2).unsqueeze(4).to_broadcast([P, 2, MAX_HEADS, PAIRS, 2]),
+        )
+        sin_heads = sin_sb[:].unsqueeze(2).to_broadcast([P, 2, MAX_HEADS, PAIRS])
+        nc.vector.tensor_scalar_mul(out=sin_table[:, 0], in0=sin_heads, scalar1=-1.0)
+        nc.vector.tensor_copy(out=sin_table[:, 1], in_=sin_heads)
+
+        w_grouped = {}
+        acc = {}
+
+        def regroup(u):
+            n, g = divmod(u, PASSES)
+            if g == 0:
+                grouped = first_pool.tile([P, BANK, PACK], BF16, name="w_first", align_bytes=64)
+                split = BANK - GPSIMD_COLUMNS
+                nc.gpsimd.tensor_scalar(
+                    out=grouped[:, split:BANK, :],
+                    in0=w_raw[u][:, :, split:BANK].rearrange("p j c -> p c j"),
+                    scalar1=1.0,
+                    scalar2=0.0,
+                    op0=MULT,
+                    op1=ADD,
+                )
+                nc.scalar.copy(
+                    out=grouped[:, 0:split, :].rearrange("p (c i) j -> p c j i", i=RUN),
+                    in_=w_raw[u][:, :, 0:split].rearrange("p j (c i) -> p c j i", i=RUN),
+                )
+            else:
+                grouped = grouped_pool.tile([P, BANK, PACK], BF16, name="w_grouped", align_bytes=64)
+                dst = grouped[:].rearrange("p (c i) j -> p c j i", i=RUN)
+                src = w_raw[u][:].rearrange("p j (c i) -> p c j i", i=RUN)
+                if n == 0 and g % 2 == 1:
+                    nc.vector.tensor_copy(out=dst, in_=src)
+                else:
+                    nc.scalar.copy(out=dst, in_=src)
+            w_grouped[u] = grouped
+
+        def prepare(u):
+            if u + 1 < UNITS:
+                regroup(u + 1)
+            codes = codes_pool.tile([P, BANK], U32, name="w_codes", align_bytes=64)
+            scales = codes_pool.tile([P, BANK], U8, name="w_scales", align_bytes=64)
+            nc.vector.quantize_mx(
+                out=codes[:].bitcast(FP8X4),
+                scales=scales[:],
+                in_=w_grouped[u][:].rearrange("p c j -> p (c j)"),
+            )
+            n, g = divmod(u, PASSES)
+            for t in range(TOKEN_TILES):
+                if g == 0:
+                    acc[(n, t)] = psum.tile([P, BANK], F32, name="acc", tag="bank")
+                nc.tensor.matmul_mx(
+                    out=acc[(n, t)][:],
+                    lhsT=x_codes[t][:, g * P : (g + 1) * P].bitcast(FP8X4),
+                    lhsT_scale=x_scales[t][:, g * P : (g + 1) * P],
+                    rhs=codes[:].bitcast(FP8X4),
+                    rhs_scale=scales[:],
+                    start=(g == 0),
+                    stop=(g == PASSES - 1),
+                )
+
+        q_tiles = {}
+        products = {}
+
+        def add_bias(n):
+            q_tile = q_pool.tile([P, TOKEN_TILES, Q_WIDTH], F32, name="q_tile")
+            for t in range(TOKEN_TILES):
+                nc.vector.tensor_tensor(
+                    out=q_tile[:, t, 0:BANK],
+                    in0=acc[(n, t)][:],
+                    in1=bias_sb[:, first_column(n) : first_column(n) + BANK],
+                    op=ADD,
+                )
+            q_tiles[n] = q_tile
+
+        def rotated_view(n):
+            first = (NOPE - first_column(n)) % HEAD
+            heads = (BANK - first + NOPE) // HEAD
+            view = q_tiles[n][:, :, first : first + heads * HEAD].rearrange(
+                "p (s a) (h d) -> p s a h d", a=2, d=HEAD
+            )
+            return heads, view[:, :, :, :, 0:ROPE].rearrange("p s a h (j e) -> p s a h j e", e=2)
+
+        def rotation_products(n):
+            heads, pairs = rotated_view(n)
+            by_cos = q_pool.tile([P, 2, 2, MAX_HEADS, PAIRS, 2], F32, name="by_cos")
+            by_sin = q_pool.tile([P, 2, 2, 2, MAX_HEADS, PAIRS], F32, name="by_sin")
+            nc.vector.tensor_tensor(
+                out=by_cos[:, :, :, 0:heads],
+                in0=pairs,
+                in1=cos_table[:, :, 0:heads].unsqueeze(1).to_broadcast([P, 2, 2, heads, PAIRS, 2]),
+                op=MULT,
+            )
+            for e in range(2):
+                nc.vector.tensor_tensor(
+                    out=by_sin[:, e, :, :, 0:heads, :],
+                    in0=pairs[:, :, :, :, :, 1 - e],
+                    in1=sin_table[:, e, :, 0:heads, :]
+                    .unsqueeze(1)
+                    .to_broadcast([P, 2, 2, heads, PAIRS]),
+                    op=MULT,
+                )
+            products[n] = (by_cos, by_sin)
+
+        def rotation_sum_and_store(n):
+            heads, pairs = rotated_view(n)
+            by_cos, by_sin = products[n]
+            nc.vector.tensor_tensor(
+                out=pairs,
+                in0=by_cos[:, :, :, 0:heads],
+                in1=by_sin[:, :, :, :, 0:heads, :].rearrange("p e s a h j -> p s a h j e"),
+                op=ADD,
+            )
+            nc.sync.dma_start(
+                out=out_rows[:, first_column(n) : first_column(n) + BANK].rearrange(
+                    "(t p) c -> p t c", p=P
+                ),
+                in_=q_tiles[n][:, :, 0:BANK],
+            )
+
+        regroup(0)
+        for n in range(PANELS + 1):
+            if 1 <= n and n - 1 + PANELS_AHEAD < PANELS:
+                load_panel(n - 1 + PANELS_AHEAD)
+            if n < PANELS:
+                prepare(n * PASSES)
+            if n >= 1:
+                add_bias(n - 1)
+            if n < PANELS:
+                prepare(n * PASSES + 1)
+            if n >= 1:
+                rotation_products(n - 1)
+            if n < PANELS:
+                prepare(n * PASSES + 2)
+                prepare(n * PASSES + 3)
+            if n >= 1:
+                rotation_sum_and_store(n - 1)

@@ -22,22 +22,22 @@ ROPE = 64
 PAIRS = ROPE // 2
 COLS = 16 * HEAD
 BANK = 512
-PSUM_BANKS = 8
+BANK_BF = 2 * BANK
+WIDE = 2 * BANK
 
 TOKEN_TILES = TOKENS // P
 PASSES = DIM // K_PASS
 PANELS = COLS // BANK
-UNITS = PANELS * PASSES
 
 MAX_HEADS = 3
 Q_WIDTH = BANK + NOPE
 
-PANELS_AHEAD = 4
-GROUPED_AHEAD = 4
-CODES_AHEAD = 6
-RESULT_TILES = 3
-
-GPSIMD_COLUMNS = 320
+RAW_TILES = 10
+GROUPED_TILES = 6
+CODES_TILES = 6
+RESULT_TILES = 4
+ACC_BANKS = 5
+WORK_BANKS = 3
 RUN = 4
 
 FLOPS = 2 * TOKENS * DIM * COLS
@@ -55,12 +55,13 @@ def tile_mla_pb_kernel(tc, x, wq_w, wq_b, cos, sin, out):
     with ExitStack() as stack:
         const = stack.enter_context(tc.tile_pool(name="const", bufs=1))
         x_pool = stack.enter_context(tc.tile_pool(name="x_pool", bufs=TOKEN_TILES))
-        raw_pool = stack.enter_context(tc.tile_pool(name="raw_pool", bufs=PANELS_AHEAD * PASSES))
-        grouped_pool = stack.enter_context(tc.tile_pool(name="grouped_pool", bufs=GROUPED_AHEAD))
-        first_pool = stack.enter_context(tc.tile_pool(name="first_pool", bufs=1))
-        codes_pool = stack.enter_context(tc.tile_pool(name="codes_pool", bufs=CODES_AHEAD))
+        raw_pool = stack.enter_context(tc.tile_pool(name="raw_pool", bufs=RAW_TILES))
+        grouped_pool = stack.enter_context(tc.tile_pool(name="grouped_pool", bufs=GROUPED_TILES))
+        codes_pool = stack.enter_context(tc.tile_pool(name="codes_pool", bufs=CODES_TILES))
         q_pool = stack.enter_context(tc.tile_pool(name="q_pool", bufs=RESULT_TILES))
-        psum = stack.enter_context(tc.psum_pool(name="psum", bufs=PSUM_BANKS))
+        product_pool = stack.enter_context(tc.tile_pool(name="product_pool", bufs=2))
+        acc_psum = stack.enter_context(tc.psum_pool(name="acc_psum", bufs=ACC_BANKS))
+        work_psum = stack.enter_context(tc.psum_pool(name="work_psum", bufs=WORK_BANKS))
 
         identity = const.tile([P, P], F32, name="identity")
         make_identity(nc, identity[:])
@@ -68,19 +69,6 @@ def tile_mla_pb_kernel(tc, x, wq_w, wq_b, cos, sin, out):
         make_identity(nc, identity_bf[:])
 
         stack.enter_context(tc.manual_schedule())
-
-        w_raw = {}
-
-        def load_panel(n):
-            for g in range(PASSES):
-                w_tile = raw_pool.tile([P, PACK, BANK], BF16, name="w_raw")
-                nc.sync.dma_start(
-                    out=w_tile[:],
-                    in_=wq_w[
-                        g * K_PASS : (g + 1) * K_PASS, first_column(n) : first_column(n) + BANK
-                    ].rearrange("(p j) c -> p j c", j=PACK),
-                )
-                w_raw[n * PASSES + g] = w_tile
 
         bias_rows = const.tile([P, BANK], BF16, name="bias_rows")
         nc.vector.memset(bias_rows[:].bitcast(F32), 0.0)
@@ -90,27 +78,59 @@ def tile_mla_pb_kernel(tc, x, wq_w, wq_b, cos, sin, out):
         nc.scalar.dma_start(out=cos_sb[:], in_=cos.rearrange("(a p) j -> p a j", p=P))
         nc.scalar.dma_start(out=sin_sb[:], in_=sin.rearrange("(a p) j -> p a j", p=P))
 
+        w_raw = {}
         x_raw = []
-        for t in range(TOKEN_TILES):
+
+        def w_rows(g, first, width):
+            return wq_w[g * K_PASS : (g + 1) * K_PASS, first : first + width].rearrange(
+                "(p j) c -> p j c", j=PACK
+            )
+
+        def load_half(n, g):
+            pair, half = divmod(n, 2)
+            if half == 0:
+                w_tile = raw_pool.tile([P, PACK, WIDE], BF16, name="w_raw")
+                w_raw[(pair, g)] = w_tile
+            lo = (1 - half) * BANK
+            nc.sync.dma_start(
+                out=w_raw[(pair, g)][:, :, lo : lo + BANK], in_=w_rows(g, first_column(n), BANK)
+            )
+
+        def load_pair(pair, g):
+            w_tile = raw_pool.tile([P, PACK, WIDE], BF16, name="w_raw")
+            w_raw[(pair, g)] = w_tile
+            nc.sync.dma_start(out=w_tile[:], in_=w_rows(g, first_column(2 * pair + 1), WIDE))
+
+        def load_x(t):
             x_tile = x_pool.tile([P, DIM], BF16, name="x_raw")
             nc.sync.dma_start(out=x_tile[:], in_=x_rows[t * P : (t + 1) * P, :])
             x_raw.append(x_tile)
 
-        for n in range(PANELS_AHEAD):
-            load_panel(n)
+        for g in range(PASSES):
+            load_half(0, g)
+            load_x(g)
+        for g in range(PASSES):
+            load_half(1, g)
+        for pair in (1, 2):
+            for g in range(PASSES):
+                load_pair(pair, g)
 
-        bias_sb = const.tile([P, COLS], F32, name="bias_sb")
+        bias_sb = const.tile([P, COLS], BF16, name="bias_sb")
 
-        def spread_bias(c):
-            spread = psum.tile([P, BANK], F32, name="spread", tag="bank")
-            nc.tensor.matmul(
-                out=spread[:],
-                lhsT=identity_bf[:, c : c + 1].to_broadcast([P, P]),
-                rhs=bias_rows[:],
-                start=True,
-                stop=True,
+        def spread_bias(b):
+            spread = work_psum.tile([P, BANK_BF], BF16, name="spread", tag="work")
+            for i in range(2):
+                c = 2 * b + i
+                nc.tensor.matmul(
+                    out=spread[:, i * BANK : (i + 1) * BANK],
+                    lhsT=identity_bf[:, c : c + 1].to_broadcast([P, P]),
+                    rhs=bias_rows[:],
+                    start=True,
+                    stop=True,
+                )
+            nc.vector.tensor_copy(
+                out=bias_sb[:, b * BANK_BF : (b + 1) * BANK_BF], in_=spread[:]
             )
-            nc.vector.tensor_copy(out=bias_sb[:, c * BANK : (c + 1) * BANK], in_=spread[:])
 
         x_grouped = []
         x_codes = []
@@ -123,7 +143,7 @@ def tile_mla_pb_kernel(tc, x, wq_w, wq_b, cos, sin, out):
                 "p (g r u) -> p g r u", g=PASSES, u=2
             )
             for half in range(2):
-                flipped = psum.tile([P, 2, 2, P], F32, name="flipped", tag="bank")
+                flipped = work_psum.tile([P, 2, 2, P], F32, name="flipped", tag="work")
                 for gg in range(2):
                     for u in range(2):
                         first_word = (2 * half + gg) * 2 * P
@@ -147,102 +167,128 @@ def tile_mla_pb_kernel(tc, x, wq_w, wq_b, cos, sin, out):
             x_codes.append(codes)
             x_scales.append(scales)
 
-        for t in range(TOKEN_TILES):
-            for c in range(2 * t, min(2 * t + 2, PANELS)):
-                spread_bias(c)
-            x_flip(t)
-            x_quantise(t)
-
-        cos_table = const.tile([P, 2, MAX_HEADS, PAIRS, 2], BF16, name="cos_table")
-        sin_table = const.tile([P, 2, 2, MAX_HEADS, PAIRS], BF16, name="sin_table")
-        nc.vector.tensor_copy(
-            out=cos_table[:],
-            in_=cos_sb[:].unsqueeze(2).unsqueeze(4).to_broadcast([P, 2, MAX_HEADS, PAIRS, 2]),
-        )
-        sin_heads = sin_sb[:].unsqueeze(2).to_broadcast([P, 2, MAX_HEADS, PAIRS])
-        nc.vector.tensor_scalar_mul(out=sin_table[:, 0], in0=sin_heads, scalar1=-1.0)
-        nc.vector.tensor_copy(out=sin_table[:, 1], in_=sin_heads)
-
         w_grouped = {}
+        w_codes = {}
         acc = {}
 
-        def regroup(u):
-            n, g = divmod(u, PASSES)
-            if g == 0:
-                grouped = first_pool.tile([P, BANK, PACK], BF16, name="w_first", align_bytes=64)
-                split = BANK - GPSIMD_COLUMNS
-                nc.gpsimd.tensor_scalar(
-                    out=grouped[:, split:BANK, :],
-                    in0=w_raw[u][:, :, split:BANK].rearrange("p j c -> p c j"),
-                    scalar1=1.0,
-                    scalar2=0.0,
-                    op0=MULT,
-                    op1=ADD,
-                )
-                nc.scalar.copy(
-                    out=grouped[:, 0:split, :].rearrange("p (c i) j -> p c j i", i=RUN),
-                    in_=w_raw[u][:, :, 0:split].rearrange("p j (c i) -> p c j i", i=RUN),
-                )
+        def mode(n, g):
+            if g == 0 or (g == 2 and n in (0, 3)):
+                return "tensor"
+            if n == 0 or (g == 1 and n in (1, 3)):
+                return "vector"
+            return "scalar"
+
+        def unit_view(n, g):
+            pair, half = divmod(n, 2)
+            lo = (1 - half) * BANK
+            return w_raw[(pair, g)][:, :, lo : lo + BANK]
+
+        mixed = {}
+
+        def mix(n, g):
+            if mode(n, g) != "tensor":
+                return
+            view = unit_view(n, g)
+            tiles = []
+            for h in range(2):
+                bank = work_psum.tile([P, BANK_BF], BF16, name="mixed", tag="work")
+                for i in range(2):
+                    lo = (2 * h + i) * P
+                    nc.tensor.matmul(
+                        out=bank[:, i * BANK : (i + 1) * BANK],
+                        lhsT=identity_bf[:],
+                        rhs=view[:, :, lo : lo + P].rearrange("p j c -> p c j"),
+                        start=True,
+                        stop=True,
+                    )
+                tiles.append(bank)
+            mixed[(n, g)] = tiles
+
+        def regroup(n, g):
+            grouped = grouped_pool.tile([P, BANK, PACK], BF16, name="w_grouped", align_bytes=64)
+            kind = mode(n, g)
+            if kind == "tensor":
+                flat = grouped[:].rearrange("p c j -> p (c j)").bitcast(F32)
+                for h in range(2):
+                    nc.scalar.copy(
+                        out=flat[:, h * BANK : (h + 1) * BANK],
+                        in_=mixed[(n, g)][h][:].bitcast(F32),
+                    )
             else:
-                grouped = grouped_pool.tile([P, BANK, PACK], BF16, name="w_grouped", align_bytes=64)
                 dst = grouped[:].rearrange("p (c i) j -> p c j i", i=RUN)
-                src = w_raw[u][:].rearrange("p j (c i) -> p c j i", i=RUN)
-                if n == 0 and g % 2 == 1:
+                src = unit_view(n, g).rearrange("p j (c i) -> p c j i", i=RUN)
+                if kind == "vector":
                     nc.vector.tensor_copy(out=dst, in_=src)
                 else:
                     nc.scalar.copy(out=dst, in_=src)
-            w_grouped[u] = grouped
+            w_grouped[(n, g)] = grouped
 
-        def prepare(u):
-            if u + 1 < UNITS:
-                regroup(u + 1)
+        def quantise(n, g):
             codes = codes_pool.tile([P, BANK], U32, name="w_codes", align_bytes=64)
             scales = codes_pool.tile([P, BANK], U8, name="w_scales", align_bytes=64)
             nc.vector.quantize_mx(
                 out=codes[:].bitcast(FP8X4),
                 scales=scales[:],
-                in_=w_grouped[u][:].rearrange("p c j -> p (c j)"),
+                in_=w_grouped[(n, g)][:].rearrange("p c j -> p (c j)"),
             )
-            n, g = divmod(u, PASSES)
-            for t in range(TOKEN_TILES):
-                if g == 0:
-                    acc[(n, t)] = psum.tile([P, BANK], F32, name="acc", tag="bank")
-                nc.tensor.matmul_mx(
-                    out=acc[(n, t)][:],
-                    lhsT=x_codes[t][:, g * P : (g + 1) * P].bitcast(FP8X4),
-                    lhsT_scale=x_scales[t][:, g * P : (g + 1) * P],
-                    rhs=codes[:].bitcast(FP8X4),
-                    rhs_scale=scales[:],
-                    start=(g == 0),
-                    stop=(g == PASSES - 1),
-                )
+            w_codes[(n, g)] = (codes, scales)
+
+        def multiply(n, g, t):
+            codes, scales = w_codes[(n, g)]
+            if g == 0:
+                acc[(n, t)] = acc_psum.tile([P, BANK], F32, name="acc", tag="bank")
+            nc.tensor.matmul_mx(
+                out=acc[(n, t)][:],
+                lhsT=x_codes[t][:, g * P : (g + 1) * P].bitcast(FP8X4),
+                lhsT_scale=x_scales[t][:, g * P : (g + 1) * P],
+                rhs=codes[:].bitcast(FP8X4),
+                rhs_scale=scales[:],
+                start=(g == 0),
+                stop=(g == PASSES - 1),
+            )
 
         q_tiles = {}
         products = {}
 
-        def add_bias(n):
-            q_tile = q_pool.tile([P, TOKEN_TILES, Q_WIDTH], F32, name="q_tile")
-            for t in range(TOKEN_TILES):
-                nc.vector.tensor_tensor(
-                    out=q_tile[:, t, 0:BANK],
-                    in0=acc[(n, t)][:],
-                    in1=bias_sb[:, first_column(n) : first_column(n) + BANK],
-                    op=ADD,
-                )
-            q_tiles[n] = q_tile
+        def add_bias(n, t):
+            if t == 0:
+                q_tile = q_pool.tile([P, TOKEN_TILES, Q_WIDTH], F32, name="q_tile")
+                q_tiles[n] = q_tile
+            nc.vector.tensor_tensor(
+                out=q_tiles[n][:, t, 0:BANK],
+                in0=acc[(n, t)][:],
+                in1=bias_sb[:, first_column(n) : first_column(n) + BANK],
+                op=ADD,
+            )
 
-        def rotated_view(n):
+        def heads_of(n):
             first = (NOPE - first_column(n)) % HEAD
-            heads = (BANK - first + NOPE) // HEAD
+            return first, (BANK - first + NOPE) // HEAD
+
+        def rotated_view(n, s):
+            first, heads = heads_of(n)
+            view = q_tiles[n][:, 2 * s : 2 * s + 2, first : first + heads * HEAD].rearrange(
+                "p a (h d) -> p a h d", d=HEAD
+            )
+            return view[:, :, :, 0:ROPE].rearrange("p a h (j e) -> p a h j e", e=2)
+
+        def rotated_both(n):
+            first, heads = heads_of(n)
             view = q_tiles[n][:, :, first : first + heads * HEAD].rearrange(
                 "p (s a) (h d) -> p s a h d", a=2, d=HEAD
             )
-            return heads, view[:, :, :, :, 0:ROPE].rearrange("p s a h (j e) -> p s a h j e", e=2)
+            return view[:, :, :, :, 0:ROPE].rearrange("p s a h (j e) -> p s a h j e", e=2)
+
+        def product_tiles(n):
+            by_cos = product_pool.tile([P, 2, 2, MAX_HEADS, PAIRS, 2], F32, name="by_cos")
+            by_sin = product_pool.tile([P, 2, 2, 2, MAX_HEADS, PAIRS], F32, name="by_sin")
+            products[n] = (by_cos, by_sin)
 
         def rotation_products(n):
-            heads, pairs = rotated_view(n)
-            by_cos = q_pool.tile([P, 2, 2, MAX_HEADS, PAIRS, 2], F32, name="by_cos")
-            by_sin = q_pool.tile([P, 2, 2, 2, MAX_HEADS, PAIRS], F32, name="by_sin")
+            product_tiles(n)
+            by_cos, by_sin = products[n]
+            heads = heads_of(n)[1]
+            pairs = rotated_both(n)
             nc.vector.tensor_tensor(
                 out=by_cos[:, :, :, 0:heads],
                 in0=pairs,
@@ -258,38 +304,143 @@ def tile_mla_pb_kernel(tc, x, wq_w, wq_b, cos, sin, out):
                     .to_broadcast([P, 2, 2, heads, PAIRS]),
                     op=MULT,
                 )
-            products[n] = (by_cos, by_sin)
 
-        def rotation_sum_and_store(n):
-            heads, pairs = rotated_view(n)
+        def rotation_sum(n, engine):
             by_cos, by_sin = products[n]
-            nc.vector.tensor_tensor(
-                out=pairs,
+            heads = heads_of(n)[1]
+            engine.tensor_tensor(
+                out=rotated_both(n),
                 in0=by_cos[:, :, :, 0:heads],
                 in1=by_sin[:, :, :, :, 0:heads, :].rearrange("p e s a h j -> p s a h j e"),
                 op=ADD,
             )
-            nc.sync.dma_start(
-                out=out_rows[:, first_column(n) : first_column(n) + BANK].rearrange(
-                    "(t p) c -> p t c", p=P
-                ),
-                in_=q_tiles[n][:, :, 0:BANK],
+
+        def batch_cos(n, s):
+            by_cos = products[n][0]
+            heads = heads_of(n)[1]
+            nc.vector.tensor_tensor(
+                out=by_cos[:, s, :, 0:heads],
+                in0=rotated_view(n, s),
+                in1=cos_table[:, :, 0:heads],
+                op=MULT,
             )
 
-        regroup(0)
-        for n in range(PANELS + 1):
-            if 1 <= n and n - 1 + PANELS_AHEAD < PANELS:
-                load_panel(n - 1 + PANELS_AHEAD)
-            if n < PANELS:
-                prepare(n * PASSES)
-            if n >= 1:
-                add_bias(n - 1)
-            if n < PANELS:
-                prepare(n * PASSES + 1)
-            if n >= 1:
-                rotation_products(n - 1)
-            if n < PANELS:
-                prepare(n * PASSES + 2)
-                prepare(n * PASSES + 3)
-            if n >= 1:
-                rotation_sum_and_store(n - 1)
+        def batch_sin(n, s):
+            by_sin = products[n][1]
+            heads = heads_of(n)[1]
+            pairs = rotated_view(n, s)
+            for e in range(2):
+                nc.vector.tensor_tensor(
+                    out=by_sin[:, e, s, :, 0:heads, :],
+                    in0=pairs[:, :, :, :, 1 - e],
+                    in1=sin_table[:, e, :, 0:heads, :],
+                    op=MULT,
+                )
+
+        def batch_sum(n, s):
+            by_cos, by_sin = products[n]
+            heads = heads_of(n)[1]
+            nc.vector.tensor_tensor(
+                out=rotated_view(n, s),
+                in0=by_cos[:, s, :, 0:heads],
+                in1=by_sin[:, :, s, :, 0:heads, :].rearrange("p e a h j -> p a h j e"),
+                op=ADD,
+            )
+
+        def store(n, first_tile, tiles):
+            rows = slice(first_tile * P, (first_tile + tiles) * P)
+            nc.sync.dma_start(
+                out=out_rows[rows, first_column(n) : first_column(n) + BANK].rearrange(
+                    "(t p) c -> p t c", p=P
+                ),
+                in_=q_tiles[n][:, first_tile : first_tile + tiles, 0:BANK],
+            )
+
+        for b in range(PANELS // 2):
+            spread_bias(b)
+        cos_table = const.tile([P, 2, MAX_HEADS, PAIRS, 2], BF16, name="cos_table")
+        sin_table = const.tile([P, 2, 2, MAX_HEADS, PAIRS], BF16, name="sin_table")
+        nc.vector.tensor_copy(
+            out=cos_table[:],
+            in_=cos_sb[:].unsqueeze(2).unsqueeze(4).to_broadcast([P, 2, MAX_HEADS, PAIRS, 2]),
+        )
+        sin_heads = sin_sb[:].unsqueeze(2).to_broadcast([P, 2, MAX_HEADS, PAIRS])
+        nc.vector.tensor_scalar_mul(out=sin_table[:, 0], in0=sin_heads, scalar1=-1.0)
+        nc.vector.tensor_copy(out=sin_table[:, 1], in_=sin_heads)
+
+        order = [(n, g) for n in range(1, PANELS) for g in range(PASSES)]
+        MIX_AHEAD, SCALAR_AHEAD, VECTOR_AHEAD = 4, 3, 1
+
+        def ahead(units, k, step, kinds=("tensor", "scalar", "vector")):
+            if k < len(units) and mode(units[k][0], units[k][1]) in kinds:
+                step(units[k][0], units[k][1])
+
+        def multiply_all(pairs):
+            for g, t in pairs:
+                multiply(0, g, t)
+
+        def prepare(n, g):
+            mix(n, g)
+            regroup(n, g)
+
+        prepare(0, 0)
+        x_flip(0)
+        quantise(0, 0)
+        prepare(0, 1)
+        x_quantise(0)
+        quantise(0, 1)
+        x_flip(1)
+        prepare(0, 2)
+        x_flip(2)
+        x_quantise(1)
+        multiply_all([(0, 0), (1, 0), (0, 1), (1, 1)])
+        quantise(0, 2)
+        prepare(0, 3)
+        x_quantise(2)
+        quantise(0, 3)
+        x_flip(3)
+        ahead(order, 0, mix)
+        ahead(order, 0, regroup, ("tensor", "scalar"))
+        multiply_all([(2, 0), (2, 1), (0, 2), (1, 2), (2, 2)])
+        x_quantise(3)
+        for k in range(VECTOR_AHEAD):
+            ahead(order, k, regroup, ("vector",))
+        multiply_all([(3, 0), (3, 1), (3, 2), (0, 3), (1, 3), (2, 3), (3, 3)])
+        for k in range(1, MIX_AHEAD):
+            ahead(order, k, mix)
+        for k in range(1, SCALAR_AHEAD):
+            ahead(order, k, regroup, ("tensor", "scalar"))
+
+        last = PANELS - 1
+        for k, (n, g) in enumerate(order):
+            ahead(order, k + MIX_AHEAD, mix)
+            ahead(order, k + SCALAR_AHEAD, regroup, ("tensor", "scalar"))
+            ahead(order, k + VECTOR_AHEAD, regroup, ("vector",))
+            quantise(n, g)
+            if g == 0:
+                if n >= 2:
+                    rotation_products(n - 2)
+                    rotation_sum(n - 2, nc.gpsimd)
+                    store(n - 2, 0, TOKEN_TILES)
+                for t in range(TOKEN_TILES):
+                    add_bias(n - 1, t)
+            if n == last:
+                if g == 1:
+                    rotation_products(n - 1)
+                if g == 3:
+                    rotation_sum(n - 1, nc.vector)
+                    store(n - 1, 0, TOKEN_TILES)
+            for t in range(TOKEN_TILES):
+                multiply(n, g, t)
+
+        for t in range(TOKEN_TILES):
+            add_bias(last, t)
+        product_tiles(last)
+        batch_cos(last, 0)
+        batch_sin(last, 0)
+        batch_cos(last, 1)
+        batch_sum(last, 0)
+        store(last, 0, 2)
+        batch_sin(last, 1)
+        batch_sum(last, 1)
+        store(last, 2, 2)

@@ -32,7 +32,8 @@ PANELS = COLS // BANK
 MAX_HEADS = 3
 Q_WIDTH = BANK + NOPE
 
-RAW_TILES = 10
+HALF_TILES = 8
+RAW_TILES = 7
 GROUPED_TILES = 6
 CODES_TILES = 6
 RESULT_TILES = 4
@@ -56,6 +57,7 @@ def tile_mla_pb_kernel(tc, x, wq_w, wq_b, cos, sin, out):
         const = stack.enter_context(tc.tile_pool(name="const", bufs=1))
         x_pool = stack.enter_context(tc.tile_pool(name="x_pool", bufs=TOKEN_TILES))
         raw_pool = stack.enter_context(tc.tile_pool(name="raw_pool", bufs=RAW_TILES))
+        half_pool = stack.enter_context(tc.tile_pool(name="half_pool", bufs=HALF_TILES))
         grouped_pool = stack.enter_context(tc.tile_pool(name="grouped_pool", bufs=GROUPED_TILES))
         codes_pool = stack.enter_context(tc.tile_pool(name="codes_pool", bufs=CODES_TILES))
         q_pool = stack.enter_context(tc.tile_pool(name="q_pool", bufs=RESULT_TILES))
@@ -86,20 +88,16 @@ def tile_mla_pb_kernel(tc, x, wq_w, wq_b, cos, sin, out):
                 "(p j) c -> p j c", j=PACK
             )
 
-        def load_half(n, g):
-            pair, half = divmod(n, 2)
-            if half == 0:
-                w_tile = raw_pool.tile([P, PACK, WIDE], BF16, name="w_raw")
-                w_raw[(pair, g)] = w_tile
-            lo = (1 - half) * BANK
-            nc.sync.dma_start(
-                out=w_raw[(pair, g)][:, :, lo : lo + BANK], in_=w_rows(g, first_column(n), BANK)
-            )
+        def load_panel(n, g):
+            w_tile = half_pool.tile([P, PACK, BANK], BF16, name="w_half")
+            nc.sync.dma_start(out=w_tile[:], in_=w_rows(g, first_column(n), BANK))
+            w_raw[(n, g)] = w_tile[:]
 
-        def load_pair(pair, g):
+        def load_pair(n, g):
             w_tile = raw_pool.tile([P, PACK, WIDE], BF16, name="w_raw")
-            w_raw[(pair, g)] = w_tile
-            nc.sync.dma_start(out=w_tile[:], in_=w_rows(g, first_column(2 * pair + 1), WIDE))
+            nc.sync.dma_start(out=w_tile[:], in_=w_rows(g, first_column(n + 1), WIDE))
+            w_raw[(n, g)] = w_tile[:, :, BANK:WIDE]
+            w_raw[(n + 1, g)] = w_tile[:, :, 0:BANK]
 
         def load_x(t):
             x_tile = x_pool.tile([P, DIM], BF16, name="x_raw")
@@ -107,13 +105,13 @@ def tile_mla_pb_kernel(tc, x, wq_w, wq_b, cos, sin, out):
             x_raw.append(x_tile)
 
         for g in range(PASSES):
-            load_half(0, g)
+            load_panel(0, g)
             load_x(g)
         for g in range(PASSES):
-            load_half(1, g)
-        for pair in (1, 2):
+            load_panel(1, g)
+        for n in (2, 4):
             for g in range(PASSES):
-                load_pair(pair, g)
+                load_pair(n, g)
 
         bias_sb = const.tile([P, COLS], BF16, name="bias_sb")
 
@@ -174,21 +172,16 @@ def tile_mla_pb_kernel(tc, x, wq_w, wq_b, cos, sin, out):
         def mode(n, g):
             if g == 0 or (g == 2 and n in (0, 3)):
                 return "tensor"
-            if n == 0 or (g == 1 and n in (1, 3)):
+            if n == 0 or (g == 1 and n == 1):
                 return "vector"
             return "scalar"
-
-        def unit_view(n, g):
-            pair, half = divmod(n, 2)
-            lo = (1 - half) * BANK
-            return w_raw[(pair, g)][:, :, lo : lo + BANK]
 
         mixed = {}
 
         def mix(n, g):
             if mode(n, g) != "tensor":
                 return
-            view = unit_view(n, g)
+            view = w_raw[(n, g)]
             tiles = []
             for h in range(2):
                 bank = work_psum.tile([P, BANK_BF], BF16, name="mixed", tag="work")
@@ -216,7 +209,7 @@ def tile_mla_pb_kernel(tc, x, wq_w, wq_b, cos, sin, out):
                     )
             else:
                 dst = grouped[:].rearrange("p (c i) j -> p c j i", i=RUN)
-                src = unit_view(n, g).rearrange("p j (c i) -> p c j i", i=RUN)
+                src = w_raw[(n, g)].rearrange("p j (c i) -> p c j i", i=RUN)
                 if kind == "vector":
                     nc.vector.tensor_copy(out=dst, in_=src)
                 else:
@@ -305,10 +298,10 @@ def tile_mla_pb_kernel(tc, x, wq_w, wq_b, cos, sin, out):
                     op=MULT,
                 )
 
-        def rotation_sum(n, engine):
+        def rotation_sum(n):
             by_cos, by_sin = products[n]
             heads = heads_of(n)[1]
-            engine.tensor_tensor(
+            nc.vector.tensor_tensor(
                 out=rotated_both(n),
                 in0=by_cos[:, :, :, 0:heads],
                 in1=by_sin[:, :, :, :, 0:heads, :].rearrange("p e s a h j -> p s a h j e"),
@@ -418,18 +411,13 @@ def tile_mla_pb_kernel(tc, x, wq_w, wq_b, cos, sin, out):
             ahead(order, k + VECTOR_AHEAD, regroup, ("vector",))
             quantise(n, g)
             if g == 0:
-                if n >= 2:
-                    rotation_products(n - 2)
-                    rotation_sum(n - 2, nc.gpsimd)
-                    store(n - 2, 0, TOKEN_TILES)
                 for t in range(TOKEN_TILES):
                     add_bias(n - 1, t)
-            if n == last:
-                if g == 1:
-                    rotation_products(n - 1)
-                if g == 3:
-                    rotation_sum(n - 1, nc.vector)
-                    store(n - 1, 0, TOKEN_TILES)
+            if g == 1:
+                rotation_products(n - 1)
+            if g == 3:
+                rotation_sum(n - 1)
+                store(n - 1, 0, TOKEN_TILES)
             for t in range(TOKEN_TILES):
                 multiply(n, g, t)
 

@@ -34,7 +34,8 @@ Q_WIDTH = BANK + NOPE
 
 HALF_TILES = 8
 RAW_TILES = 7
-GROUPED_TILES = 6
+GROUPED_TILES = 5
+GPSIMD_COLUMNS = 320
 CODES_TILES = 6
 RESULT_TILES = 4
 ACC_BANKS = 5
@@ -59,6 +60,7 @@ def tile_mla_pb_kernel(tc, x, wq_w, wq_b, cos, sin, out):
         raw_pool = stack.enter_context(tc.tile_pool(name="raw_pool", bufs=RAW_TILES))
         half_pool = stack.enter_context(tc.tile_pool(name="half_pool", bufs=HALF_TILES))
         grouped_pool = stack.enter_context(tc.tile_pool(name="grouped_pool", bufs=GROUPED_TILES))
+        first_pool = stack.enter_context(tc.tile_pool(name="first_pool", bufs=1))
         codes_pool = stack.enter_context(tc.tile_pool(name="codes_pool", bufs=CODES_TILES))
         q_pool = stack.enter_context(tc.tile_pool(name="q_pool", bufs=RESULT_TILES))
         product_pool = stack.enter_context(tc.tile_pool(name="product_pool", bufs=2))
@@ -169,52 +171,38 @@ def tile_mla_pb_kernel(tc, x, wq_w, wq_b, cos, sin, out):
         w_codes = {}
         acc = {}
 
-        def mode(n, g):
-            if g == 0 or (g == 2 and n in (0, 3)):
-                return "tensor"
-            if n == 0 or (g == 1 and n == 1):
-                return "vector"
-            return "scalar"
+        def gpsimd_columns(n, g):
+            if g > 0 or n == 1:
+                return 0
+            return BANK // 2 if n == 0 else GPSIMD_COLUMNS
 
-        mixed = {}
+        def on_vector(n, g):
+            return g % 2 == 1 and n == 0 or (n, g) == (1, 1)
 
-        def mix(n, g):
-            if mode(n, g) != "tensor":
-                return
-            view = w_raw[(n, g)]
-            tiles = []
-            for h in range(2):
-                bank = work_psum.tile([P, BANK_BF], BF16, name="mixed", tag="work")
-                for i in range(2):
-                    lo = (2 * h + i) * P
-                    nc.tensor.matmul(
-                        out=bank[:, i * BANK : (i + 1) * BANK],
-                        lhsT=identity_bf[:],
-                        rhs=view[:, :, lo : lo + P].rearrange("p j c -> p c j"),
-                        start=True,
-                        stop=True,
-                    )
-                tiles.append(bank)
-            mixed[(n, g)] = tiles
+        def regroup_gpsimd(n, g):
+            pool = first_pool if g == 0 else grouped_pool
+            name = "w_first" if g == 0 else "w_grouped"
+            grouped = pool.tile([P, BANK, PACK], BF16, name=name, align_bytes=64)
+            w_grouped[(n, g)] = grouped
+            split = BANK - gpsimd_columns(n, g)
+            if split < BANK:
+                nc.gpsimd.tensor_scalar(
+                    out=grouped[:, split:BANK, :],
+                    in0=w_raw[(n, g)][:, :, split:BANK].rearrange("p j c -> p c j"),
+                    scalar1=1.0,
+                    scalar2=0.0,
+                    op0=MULT,
+                    op1=ADD,
+                )
 
         def regroup(n, g):
-            grouped = grouped_pool.tile([P, BANK, PACK], BF16, name="w_grouped", align_bytes=64)
-            kind = mode(n, g)
-            if kind == "tensor":
-                flat = grouped[:].rearrange("p c j -> p (c j)").bitcast(F32)
-                for h in range(2):
-                    nc.scalar.copy(
-                        out=flat[:, h * BANK : (h + 1) * BANK],
-                        in_=mixed[(n, g)][h][:].bitcast(F32),
-                    )
+            split = BANK - gpsimd_columns(n, g)
+            dst = w_grouped[(n, g)][:, 0:split, :].rearrange("p (c i) j -> p c j i", i=RUN)
+            src = w_raw[(n, g)][:, :, 0:split].rearrange("p j (c i) -> p c j i", i=RUN)
+            if on_vector(n, g):
+                nc.vector.tensor_copy(out=dst, in_=src)
             else:
-                dst = grouped[:].rearrange("p (c i) j -> p c j i", i=RUN)
-                src = w_raw[(n, g)].rearrange("p j (c i) -> p c j i", i=RUN)
-                if kind == "vector":
-                    nc.vector.tensor_copy(out=dst, in_=src)
-                else:
-                    nc.scalar.copy(out=dst, in_=src)
-            w_grouped[(n, g)] = grouped
+                nc.scalar.copy(out=dst, in_=src)
 
         def quantise(n, g):
             codes = codes_pool.tile([P, BANK], U32, name="w_codes", align_bytes=64)
@@ -362,18 +350,18 @@ def tile_mla_pb_kernel(tc, x, wq_w, wq_b, cos, sin, out):
         nc.vector.tensor_copy(out=sin_table[:, 1], in_=sin_heads)
 
         order = [(n, g) for n in range(1, PANELS) for g in range(PASSES)]
-        MIX_AHEAD, SCALAR_AHEAD, VECTOR_AHEAD = 4, 3, 1
+        SCALAR_AHEAD, VECTOR_AHEAD = 3, 1
 
-        def ahead(units, k, step, kinds=("tensor", "scalar", "vector")):
-            if k < len(units) and mode(units[k][0], units[k][1]) in kinds:
-                step(units[k][0], units[k][1])
+        def ahead(k, vector):
+            if k < len(order) and on_vector(order[k][0], order[k][1]) == vector:
+                prepare(order[k][0], order[k][1])
 
         def multiply_all(pairs):
             for g, t in pairs:
                 multiply(0, g, t)
 
         def prepare(n, g):
-            mix(n, g)
+            regroup_gpsimd(n, g)
             regroup(n, g)
 
         prepare(0, 0)
@@ -392,23 +380,19 @@ def tile_mla_pb_kernel(tc, x, wq_w, wq_b, cos, sin, out):
         x_quantise(2)
         quantise(0, 3)
         x_flip(3)
-        ahead(order, 0, mix)
-        ahead(order, 0, regroup, ("tensor", "scalar"))
+        ahead(0, False)
         multiply_all([(2, 0), (2, 1), (0, 2), (1, 2), (2, 2)])
         x_quantise(3)
         for k in range(VECTOR_AHEAD):
-            ahead(order, k, regroup, ("vector",))
+            ahead(k, True)
         multiply_all([(3, 0), (3, 1), (3, 2), (0, 3), (1, 3), (2, 3), (3, 3)])
-        for k in range(1, MIX_AHEAD):
-            ahead(order, k, mix)
         for k in range(1, SCALAR_AHEAD):
-            ahead(order, k, regroup, ("tensor", "scalar"))
+            ahead(k, False)
 
         last = PANELS - 1
         for k, (n, g) in enumerate(order):
-            ahead(order, k + MIX_AHEAD, mix)
-            ahead(order, k + SCALAR_AHEAD, regroup, ("tensor", "scalar"))
-            ahead(order, k + VECTOR_AHEAD, regroup, ("vector",))
+            ahead(k + SCALAR_AHEAD, False)
+            ahead(k + VECTOR_AHEAD, True)
             quantise(n, g)
             if g == 0:
                 for t in range(TOKEN_TILES):

@@ -261,70 +261,53 @@ def tile_mla_pb_kernel(tc, x, wq_w, wq_b, cos, sin, out):
             return view[:, :, :, :, 0:ROPE].rearrange("p s a h (j e) -> p s a h j e", e=2)
 
         def product_tiles(n):
-            by_cos = product_pool.tile([P, 2, 2, MAX_HEADS, PAIRS, 2], F32, name="by_cos")
-            by_sin = product_pool.tile([P, 2, 2, 2, MAX_HEADS, PAIRS], F32, name="by_sin")
-            products[n] = (by_cos, by_sin)
+            heads = heads_of(n)[1]
+            size = TOKEN_TILES * heads * ROPE
+            pair = []
+            for name in ("by_cos", "by_sin"):
+                flat = product_pool.tile([P, TOKEN_TILES * MAX_HEADS * ROPE], F32, name=name)
+                pair.append(
+                    flat[:, 0:size].rearrange(
+                        "p (s a h j e) -> p s a h j e", s=2, a=2, h=heads, e=2
+                    )
+                )
+            products[n] = pair
 
         def rotation_products(n):
             product_tiles(n)
-            by_cos, by_sin = products[n]
             heads = heads_of(n)[1]
-            pairs = rotated_both(n)
-            nc.vector.tensor_tensor(
-                out=by_cos[:, :, :, 0:heads],
-                in0=pairs,
-                in1=cos_table[:, :, 0:heads].unsqueeze(1).to_broadcast([P, 2, 2, heads, PAIRS, 2]),
-                op=MULT,
-            )
-            for e in range(2):
+            for product, table in zip(products[n], (cos_table, sin_table)):
                 nc.vector.tensor_tensor(
-                    out=by_sin[:, e, :, :, 0:heads, :],
-                    in0=pairs[:, :, :, :, :, 1 - e],
-                    in1=sin_table[:, e, :, 0:heads, :]
-                    .unsqueeze(1)
-                    .to_broadcast([P, 2, 2, heads, PAIRS]),
+                    out=product,
+                    in0=rotated_both(n),
+                    in1=table[:, :, 0:heads].unsqueeze(1).to_broadcast([P, 2, 2, heads, PAIRS, 2]),
                     op=MULT,
                 )
 
         def rotation_sum(n):
             by_cos, by_sin = products[n]
-            heads = heads_of(n)[1]
             nc.vector.tensor_tensor(
                 out=rotated_both(n),
-                in0=by_cos[:, :, :, 0:heads],
-                in1=by_sin[:, :, :, :, 0:heads, :].rearrange("p e s a h j -> p s a h j e"),
+                in0=by_cos,
+                in1=by_sin[:, :, :, :, :, ::-1],
                 op=ADD,
             )
 
-        def batch_cos(n, s):
-            by_cos = products[n][0]
+        def batch_product(n, s, i):
             heads = heads_of(n)[1]
             nc.vector.tensor_tensor(
-                out=by_cos[:, s, :, 0:heads],
+                out=products[n][i][:, s],
                 in0=rotated_view(n, s),
-                in1=cos_table[:, :, 0:heads],
+                in1=(cos_table, sin_table)[i][:, :, 0:heads],
                 op=MULT,
             )
 
-        def batch_sin(n, s):
-            by_sin = products[n][1]
-            heads = heads_of(n)[1]
-            pairs = rotated_view(n, s)
-            for e in range(2):
-                nc.vector.tensor_tensor(
-                    out=by_sin[:, e, s, :, 0:heads, :],
-                    in0=pairs[:, :, :, :, 1 - e],
-                    in1=sin_table[:, e, :, 0:heads, :],
-                    op=MULT,
-                )
-
         def batch_sum(n, s):
             by_cos, by_sin = products[n]
-            heads = heads_of(n)[1]
             nc.vector.tensor_tensor(
                 out=rotated_view(n, s),
-                in0=by_cos[:, s, :, 0:heads],
-                in1=by_sin[:, :, s, :, 0:heads, :].rearrange("p e a h j -> p a h j e"),
+                in0=by_cos[:, s],
+                in1=by_sin[:, s, :, :, :, ::-1],
                 op=ADD,
             )
 
@@ -340,14 +323,14 @@ def tile_mla_pb_kernel(tc, x, wq_w, wq_b, cos, sin, out):
         for b in range(PANELS // 2):
             spread_bias(b)
         cos_table = const.tile([P, 2, MAX_HEADS, PAIRS, 2], BF16, name="cos_table")
-        sin_table = const.tile([P, 2, 2, MAX_HEADS, PAIRS], BF16, name="sin_table")
+        sin_table = const.tile([P, 2, MAX_HEADS, PAIRS, 2], BF16, name="sin_table")
         nc.vector.tensor_copy(
             out=cos_table[:],
             in_=cos_sb[:].unsqueeze(2).unsqueeze(4).to_broadcast([P, 2, MAX_HEADS, PAIRS, 2]),
         )
         sin_heads = sin_sb[:].unsqueeze(2).to_broadcast([P, 2, MAX_HEADS, PAIRS])
-        nc.vector.tensor_scalar_mul(out=sin_table[:, 0], in0=sin_heads, scalar1=-1.0)
-        nc.vector.tensor_copy(out=sin_table[:, 1], in_=sin_heads)
+        nc.vector.tensor_copy(out=sin_table[:, :, :, :, 0], in_=sin_heads)
+        nc.vector.tensor_scalar_mul(out=sin_table[:, :, :, :, 1], in0=sin_heads, scalar1=-1.0)
 
         order = [(n, g) for n in range(1, PANELS) for g in range(PASSES)]
         SCALAR_AHEAD, VECTOR_AHEAD = 3, 1
@@ -408,11 +391,11 @@ def tile_mla_pb_kernel(tc, x, wq_w, wq_b, cos, sin, out):
         for t in range(TOKEN_TILES):
             add_bias(last, t)
         product_tiles(last)
-        batch_cos(last, 0)
-        batch_sin(last, 0)
-        batch_cos(last, 1)
+        batch_product(last, 0, 0)
+        batch_product(last, 0, 1)
+        batch_product(last, 1, 0)
         batch_sum(last, 0)
         store(last, 0, 2)
-        batch_sin(last, 1)
+        batch_product(last, 1, 1)
         batch_sum(last, 1)
         store(last, 2, 2)

@@ -40,7 +40,7 @@ CODES_TILES = 6
 RESULT_TILES = 4
 ACC_BANKS = 5
 WORK_BANKS = 3
-RUN = 4
+RUN = 2
 
 FLOPS = 2 * TOKENS * DIM * COLS
 

@@ -35,7 +35,7 @@ Q_WIDTH = BANK + NOPE
 HALF_TILES = 8
 RAW_TILES = 7
 GROUPED_TILES = 5
-GPSIMD_COLUMNS = 320
+GPSIMD_COLUMNS = 384
 CODES_TILES = 6
 RESULT_TILES = 4
 ACC_BANKS = 5

@@ -32,17 +32,19 @@ PANELS = COLS // BANK
 MAX_HEADS = 3
 Q_WIDTH = BANK + NOPE
 
-HALF_TILES = 8
-RAW_TILES = 7
+RAW_TILES = 10
 GROUPED_TILES = 5
 GPSIMD_COLUMNS = 384
-CODES_TILES = 6
-RESULT_TILES = 4
+CODES_TILES = 9
+RESULT_TILES = 3
 ACC_BANKS = 5
 WORK_BANKS = 3
 RUN = 2
 
 FLOPS = 2 * TOKENS * DIM * COLS
+
+
+LAST = PANELS - 1
 
 
 def first_column(n):
@@ -58,7 +60,6 @@ def tile_mla_pb_kernel(tc, x, wq_w, wq_b, cos, sin, out):
         const = stack.enter_context(tc.tile_pool(name="const", bufs=1))
         x_pool = stack.enter_context(tc.tile_pool(name="x_pool", bufs=TOKEN_TILES))
         raw_pool = stack.enter_context(tc.tile_pool(name="raw_pool", bufs=RAW_TILES))
-        half_pool = stack.enter_context(tc.tile_pool(name="half_pool", bufs=HALF_TILES))
         grouped_pool = stack.enter_context(tc.tile_pool(name="grouped_pool", bufs=GROUPED_TILES))
         first_pool = stack.enter_context(tc.tile_pool(name="first_pool", bufs=1))
         codes_pool = stack.enter_context(tc.tile_pool(name="codes_pool", bufs=CODES_TILES))
@@ -90,11 +91,6 @@ def tile_mla_pb_kernel(tc, x, wq_w, wq_b, cos, sin, out):
                 "(p j) c -> p j c", j=PACK
             )
 
-        def load_panel(n, g):
-            w_tile = half_pool.tile([P, PACK, BANK], BF16, name="w_half")
-            nc.sync.dma_start(out=w_tile[:], in_=w_rows(g, first_column(n), BANK))
-            w_raw[(n, g)] = w_tile[:]
-
         def load_pair(n, g):
             w_tile = raw_pool.tile([P, PACK, WIDE], BF16, name="w_raw")
             nc.sync.dma_start(out=w_tile[:], in_=w_rows(g, first_column(n + 1), WIDE))
@@ -107,11 +103,9 @@ def tile_mla_pb_kernel(tc, x, wq_w, wq_b, cos, sin, out):
             x_raw.append(x_tile)
 
         for g in range(PASSES):
-            load_panel(0, g)
+            load_pair(0, g)
             load_x(g)
-        for g in range(PASSES):
-            load_panel(1, g)
-        for n in (2, 4):
+        for n in range(2, PANELS, 2):
             for g in range(PASSES):
                 load_pair(n, g)
 
@@ -172,12 +166,12 @@ def tile_mla_pb_kernel(tc, x, wq_w, wq_b, cos, sin, out):
         acc = {}
 
         def gpsimd_columns(n, g):
-            if g > 0 or n == 1:
+            if g > 0:
                 return 0
-            return BANK // 2 if n == 0 else GPSIMD_COLUMNS
+            return BANK // 2 if n == 0 else 0 if n == 1 else GPSIMD_COLUMNS
 
         def on_vector(n, g):
-            return g % 2 == 1 and n == 0 or (n, g) == (1, 1)
+            return n == 0 and g > 0
 
         def regroup_gpsimd(n, g):
             pool = first_pool if g == 0 else grouped_pool
@@ -284,9 +278,9 @@ def tile_mla_pb_kernel(tc, x, wq_w, wq_b, cos, sin, out):
                     op=MULT,
                 )
 
-        def rotation_sum(n):
+        def rotation_sum(n, engine=nc.vector):
             by_cos, by_sin = products[n]
-            nc.vector.tensor_tensor(
+            engine.tensor_tensor(
                 out=rotated_both(n),
                 in0=by_cos,
                 in1=by_sin[:, :, :, :, :, ::-1],
@@ -332,70 +326,97 @@ def tile_mla_pb_kernel(tc, x, wq_w, wq_b, cos, sin, out):
         nc.vector.tensor_copy(out=sin_table[:, :, :, :, 0], in_=sin_heads)
         nc.vector.tensor_scalar_mul(out=sin_table[:, :, :, :, 1], in0=sin_heads, scalar1=-1.0)
 
-        order = [(n, g) for n in range(1, PANELS) for g in range(PASSES)]
-        SCALAR_AHEAD, VECTOR_AHEAD = 3, 1
-
-        def ahead(k, vector):
-            if k < len(order) and on_vector(order[k][0], order[k][1]) == vector:
-                prepare(order[k][0], order[k][1])
-
-        def multiply_all(pairs):
-            for g, t in pairs:
-                multiply(0, g, t)
-
         def prepare(n, g):
             regroup_gpsimd(n, g)
             regroup(n, g)
 
+        def multiply_some(n, passes, tiles):
+            for t in tiles:
+                for g in passes:
+                    multiply(n, g, t)
+
+        order = [(n, g) for n in range(2, PANELS) for g in range(PASSES)]
+        SCALAR_AHEAD = 3
+
+        def ahead(k):
+            if k < len(order):
+                prepare(order[k][0], order[k][1])
+
         prepare(0, 0)
         x_flip(0)
         quantise(0, 0)
+        prepare(1, 0)
         prepare(0, 1)
         x_quantise(0)
         quantise(0, 1)
+        quantise(1, 0)
         x_flip(1)
+        prepare(1, 1)
+        multiply_some(0, (0, 1), (0,))
         prepare(0, 2)
-        x_flip(2)
         x_quantise(1)
-        multiply_all([(0, 0), (1, 0), (0, 1), (1, 1)])
         quantise(0, 2)
+        quantise(1, 1)
+        x_flip(2)
+        multiply_some(0, (0, 1), (1,))
+        multiply_some(0, (2,), (0, 1))
+        prepare(1, 2)
         prepare(0, 3)
         x_quantise(2)
         quantise(0, 3)
+        quantise(1, 2)
         x_flip(3)
-        ahead(0, False)
-        multiply_all([(2, 0), (2, 1), (0, 2), (1, 2), (2, 2)])
+        multiply_some(0, (0, 1, 2), (2,))
+        multiply_some(0, (3,), (0, 1, 2))
+        prepare(1, 3)
         x_quantise(3)
-        for k in range(VECTOR_AHEAD):
-            ahead(k, True)
-        multiply_all([(3, 0), (3, 1), (3, 2), (0, 3), (1, 3), (2, 3), (3, 3)])
-        for k in range(1, SCALAR_AHEAD):
-            ahead(k, False)
+        multiply_some(0, range(PASSES), (3,))
+        for k in range(SCALAR_AHEAD):
+            ahead(k)
+        for t in range(TOKEN_TILES):
+            add_bias(0, t)
+        quantise(1, 3)
+        multiply_some(1, range(PASSES), range(TOKEN_TILES))
+        rotation_products(0)
 
-        last = PANELS - 1
+        last = LAST
         for k, (n, g) in enumerate(order):
-            ahead(k + SCALAR_AHEAD, False)
-            ahead(k + VECTOR_AHEAD, True)
+            ahead(k + SCALAR_AHEAD)
             quantise(n, g)
-            if g == 0:
-                for t in range(TOKEN_TILES):
-                    add_bias(n - 1, t)
-            if g == 1:
-                rotation_products(n - 1)
-            if g == 3:
+            if n == 2:
+                if g == 0:
+                    rotation_sum(0)
+                    store(0, 0, TOKEN_TILES)
+                if g == 1:
+                    for t in range(TOKEN_TILES):
+                        add_bias(1, t)
+                    rotation_products(1)
+            else:
+                if g == 0:
+                    if n == last:
+                        rotation_products(n - 2)
+                        rotation_sum(n - 2, nc.gpsimd)
+                        store(n - 2, 0, TOKEN_TILES)
+                    for t in range(TOKEN_TILES):
+                        add_bias(n - 1, t)
+                if g == 1 and n != last - 1:
+                    rotation_products(n - 1)
+            if g == 3 and n != last - 1:
                 rotation_sum(n - 1)
                 store(n - 1, 0, TOKEN_TILES)
             for t in range(TOKEN_TILES):
                 multiply(n, g, t)
 
-        for t in range(TOKEN_TILES):
-            add_bias(last, t)
         product_tiles(last)
+        add_bias(last, 0)
+        add_bias(last, 1)
         batch_product(last, 0, 0)
         batch_product(last, 0, 1)
-        batch_product(last, 1, 0)
+        add_bias(last, 2)
+        add_bias(last, 3)
         batch_sum(last, 0)
         store(last, 0, 2)
+        batch_product(last, 1, 0)
         batch_product(last, 1, 1)
         batch_sum(last, 1)
         store(last, 2, 2)

@@ -77,7 +77,6 @@ def tile_mla_pb_kernel(tc, x, wq_w, wq_b, cos, sin, out):
 
         bias_rows = const.tile([P, BANK], BF16, name="bias_rows")
         nc.vector.memset(bias_rows[:].bitcast(F32), 0.0)
-        nc.sync.dma_start(out=bias_rows[0:PANELS, :], in_=wq_b.rearrange("(c w) -> c w", w=BANK))
         cos_sb = const.tile([P, 2, PAIRS], BF16, name="cos_sb")
         sin_sb = const.tile([P, 2, PAIRS], BF16, name="sin_sb")
         nc.scalar.dma_start(out=cos_sb[:], in_=cos.rearrange("(a p) j -> p a j", p=P))
@@ -104,6 +103,10 @@ def tile_mla_pb_kernel(tc, x, wq_w, wq_b, cos, sin, out):
 
         for g in range(PASSES):
             load_pair(0, g)
+            if g == 0:
+                nc.sync.dma_start(
+                    out=bias_rows[0:PANELS, :], in_=wq_b.rearrange("(c w) -> c w", w=BANK)
+                )
             load_x(g)
         for n in range(2, PANELS, 2):
             for g in range(PASSES):
@@ -305,6 +308,16 @@ def tile_mla_pb_kernel(tc, x, wq_w, wq_b, cos, sin, out):
                 op=ADD,
             )
 
+        def tile_sum(n, t):
+            s, a = divmod(t, 2)
+            by_cos, by_sin = products[n]
+            nc.vector.tensor_tensor(
+                out=rotated_view(n, s)[:, a],
+                in0=by_cos[:, s, a],
+                in1=by_sin[:, s, a, :, :, ::-1],
+                op=ADD,
+            )
+
         def store(n, first_tile, tiles):
             rows = slice(first_tile * P, (first_tile + tiles) * P)
             nc.sync.dma_start(
@@ -314,8 +327,6 @@ def tile_mla_pb_kernel(tc, x, wq_w, wq_b, cos, sin, out):
                 in_=q_tiles[n][:, first_tile : first_tile + tiles, 0:BANK],
             )
 
-        for b in range(PANELS // 2):
-            spread_bias(b)
         cos_table = const.tile([P, 2, MAX_HEADS, PAIRS, 2], BF16, name="cos_table")
         sin_table = const.tile([P, 2, MAX_HEADS, PAIRS, 2], BF16, name="sin_table")
         nc.vector.tensor_copy(
@@ -346,29 +357,32 @@ def tile_mla_pb_kernel(tc, x, wq_w, wq_b, cos, sin, out):
         x_flip(0)
         quantise(0, 0)
         prepare(1, 0)
-        prepare(0, 1)
         x_quantise(0)
-        quantise(0, 1)
+        spread_bias(0)
+        prepare(0, 1)
         quantise(1, 0)
+        quantise(0, 1)
         x_flip(1)
         prepare(1, 1)
+        spread_bias(1)
         multiply_some(0, (0, 1), (0,))
-        prepare(0, 2)
         x_quantise(1)
-        quantise(0, 2)
+        prepare(0, 2)
         quantise(1, 1)
+        quantise(0, 2)
         x_flip(2)
+        prepare(1, 2)
+        spread_bias(2)
         multiply_some(0, (0, 1), (1,))
         multiply_some(0, (2,), (0, 1))
-        prepare(1, 2)
-        prepare(0, 3)
         x_quantise(2)
-        quantise(0, 3)
+        prepare(0, 3)
         quantise(1, 2)
+        quantise(0, 3)
         x_flip(3)
+        prepare(1, 3)
         multiply_some(0, (0, 1, 2), (2,))
         multiply_some(0, (3,), (0, 1, 2))
-        prepare(1, 3)
         x_quantise(3)
         multiply_some(0, range(PASSES), (3,))
         for k in range(SCALAR_AHEAD):
@@ -418,5 +432,6 @@ def tile_mla_pb_kernel(tc, x, wq_w, wq_b, cos, sin, out):
         store(last, 0, 2)
         batch_product(last, 1, 0)
         batch_product(last, 1, 1)
-        batch_sum(last, 1)
-        store(last, 2, 2)
+        for t in (2, 3):
+            tile_sum(last, t)
+            store(last, t, 1)

from contextlib import ExitStack

import concourse.mybir as mybir
from concourse.masks import make_identity

F32 = mybir.dt.float32
BF16 = mybir.dt.bfloat16
U32 = mybir.dt.uint32
U8 = mybir.dt.uint8
FP8X4 = mybir.dt.float8_e4m3fn_x4
ADD = mybir.AluOpType.add
MULT = mybir.AluOpType.mult

P = 128
PACK = 4
K_PASS = P * PACK
TOKENS = 512
DIM = 2048
HEAD = 192
NOPE = 128
ROPE = 64
PAIRS = ROPE // 2
COLS = 16 * HEAD
BANK = 512
BANK_BF = 2 * BANK
WIDE = 2 * BANK

TOKEN_TILES = TOKENS // P
PASSES = DIM // K_PASS
PANELS = COLS // BANK

MAX_HEADS = 3
Q_WIDTH = BANK + NOPE

RAW_TILES = 10
GROUPED_TILES = 5
GPSIMD_COLUMNS = 384
CODES_TILES = 9
RESULT_TILES = 3
ACC_BANKS = 5
WORK_BANKS = 3
RUN = 2

FLOPS = 2 * TOKENS * DIM * COLS


LAST = PANELS - 1


def first_column(n):
    return (PANELS - 1 - n) * BANK


def tile_mla_pb_kernel(tc, x, wq_w, wq_b, cos, sin, out):
    nc = tc.nc
    x_rows = x.flatten_outer_dims()
    out_rows = out.rearrange("b s h d -> (b s) (h d)")

    with ExitStack() as stack:
        const = stack.enter_context(tc.tile_pool(name="const", bufs=1))
        x_pool = stack.enter_context(tc.tile_pool(name="x_pool", bufs=TOKEN_TILES))
        raw_pool = stack.enter_context(tc.tile_pool(name="raw_pool", bufs=RAW_TILES))
        grouped_pool = stack.enter_context(tc.tile_pool(name="grouped_pool", bufs=GROUPED_TILES))
        first_pool = stack.enter_context(tc.tile_pool(name="first_pool", bufs=1))
        codes_pool = stack.enter_context(tc.tile_pool(name="codes_pool", bufs=CODES_TILES))
        q_pool = stack.enter_context(tc.tile_pool(name="q_pool", bufs=RESULT_TILES))
        product_pool = stack.enter_context(tc.tile_pool(name="product_pool", bufs=2))
        acc_psum = stack.enter_context(tc.psum_pool(name="acc_psum", bufs=ACC_BANKS))
        work_psum = stack.enter_context(tc.psum_pool(name="work_psum", bufs=WORK_BANKS))

        identity = const.tile([P, P], F32, name="identity")
        make_identity(nc, identity[:])
        identity_bf = const.tile([P, P], BF16, name="identity_bf")
        make_identity(nc, identity_bf[:])

        stack.enter_context(tc.manual_schedule())

        bias_rows = const.tile([P, BANK], BF16, name="bias_rows")
        nc.vector.memset(bias_rows[:].bitcast(F32), 0.0)
        cos_sb = const.tile([P, 2, PAIRS], BF16, name="cos_sb")
        sin_sb = const.tile([P, 2, PAIRS], BF16, name="sin_sb")
        nc.scalar.dma_start(out=cos_sb[:], in_=cos.rearrange("(a p) j -> p a j", p=P))
        nc.scalar.dma_start(out=sin_sb[:], in_=sin.rearrange("(a p) j -> p a j", p=P))

        w_raw = {}
        x_raw = []

        def w_rows(g, first, width):
            return wq_w[g * K_PASS : (g + 1) * K_PASS, first : first + width].rearrange(
                "(p j) c -> p j c", j=PACK
            )

        def load_pair(n, g):
            w_tile = raw_pool.tile([P, PACK, WIDE], BF16, name="w_raw")
            nc.sync.dma_start(out=w_tile[:], in_=w_rows(g, first_column(n + 1), WIDE))
            w_raw[(n, g)] = w_tile[:, :, BANK:WIDE]
            w_raw[(n + 1, g)] = w_tile[:, :, 0:BANK]

        def load_x(t):
            x_tile = x_pool.tile([P, DIM], BF16, name="x_raw")
            nc.sync.dma_start(out=x_tile[:], in_=x_rows[t * P : (t + 1) * P, :])
            x_raw.append(x_tile)

        for g in range(PASSES):
            load_pair(0, g)
            if g == 0:
                nc.sync.dma_start(
                    out=bias_rows[0:PANELS, :], in_=wq_b.rearrange("(c w) -> c w", w=BANK)
                )
            load_x(g)
        for n in range(2, PANELS, 2):
            for g in range(PASSES):
                load_pair(n, g)

        bias_sb = const.tile([P, COLS], BF16, name="bias_sb")

        def spread_bias(b):
            spread = work_psum.tile([P, BANK_BF], BF16, name="spread", tag="work")
            for i in range(2):
                c = 2 * b + i
                nc.tensor.matmul(
                    out=spread[:, i * BANK : (i + 1) * BANK],
                    lhsT=identity_bf[:, c : c + 1].to_broadcast([P, P]),
                    rhs=bias_rows[:],
                    start=True,
                    stop=True,
                )
            nc.vector.tensor_copy(
                out=bias_sb[:, b * BANK_BF : (b + 1) * BANK_BF], in_=spread[:]
            )

        x_grouped = []
        x_codes = []
        x_scales = []

        def x_flip(t):
            words = x_raw[t][:].bitcast(F32)
            grouped = x_pool.tile([P, PASSES * P * PACK], BF16, name="x_grouped", align_bytes=64)
            grouped_words = grouped[:].bitcast(F32).rearrange(
                "p (g r u) -> p g r u", g=PASSES, u=2
            )
            for half in range(2):
                flipped = work_psum.tile([P, 2, 2, P], F32, name="flipped", tag="work")
                for gg in range(2):
                    for u in range(2):
                        first_word = (2 * half + gg) * 2 * P
                        nc.tensor.transpose(
                            flipped[:, gg, u, :],
                            words[:, first_word + u : first_word + 2 * P : 2],
                            identity[:],
                        )
                nc.scalar.copy(
                    out=grouped_words[:, 2 * half : 2 * half + 2],
                    in_=flipped[:].rearrange("p g u r -> p g r u"),
                )
            x_grouped.append(grouped)

        def x_quantise(t):
            codes = x_pool.tile([P, PASSES * P], U32, name="x_codes", align_bytes=64)
            scales = x_pool.tile([P, PASSES * P], U8, name="x_scales", align_bytes=64)
            nc.vector.quantize_mx(
                out=codes[:].bitcast(FP8X4), scales=scales[:], in_=x_grouped[t][:]
            )
            x_codes.append(codes)
            x_scales.append(scales)

        w_grouped = {}
        w_codes = {}
        acc = {}

        def gpsimd_columns(n, g):
            if g > 0:
                return 0
            return BANK // 2 if n == 0 else 0 if n == 1 else GPSIMD_COLUMNS

        def on_vector(n, g):
            return n == 0 and g > 0

        def regroup_gpsimd(n, g):
            pool = first_pool if g == 0 else grouped_pool
            name = "w_first" if g == 0 else "w_grouped"
            grouped = pool.tile([P, BANK, PACK], BF16, name=name, align_bytes=64)
            w_grouped[(n, g)] = grouped
            split = BANK - gpsimd_columns(n, g)
            if split < BANK:
                nc.gpsimd.tensor_scalar(
                    out=grouped[:, split:BANK, :],
                    in0=w_raw[(n, g)][:, :, split:BANK].rearrange("p j c -> p c j"),
                    scalar1=1.0,
                    scalar2=0.0,
                    op0=MULT,
                    op1=ADD,
                )

        def regroup(n, g):
            split = BANK - gpsimd_columns(n, g)
            dst = w_grouped[(n, g)][:, 0:split, :].rearrange("p (c i) j -> p c j i", i=RUN)
            src = w_raw[(n, g)][:, :, 0:split].rearrange("p j (c i) -> p c j i", i=RUN)
            if on_vector(n, g):
                nc.vector.tensor_copy(out=dst, in_=src)
            else:
                nc.scalar.copy(out=dst, in_=src)

        def quantise(n, g):
            codes = codes_pool.tile([P, BANK], U32, name="w_codes", align_bytes=64)
            scales = codes_pool.tile([P, BANK], U8, name="w_scales", align_bytes=64)
            nc.vector.quantize_mx(
                out=codes[:].bitcast(FP8X4),
                scales=scales[:],
                in_=w_grouped[(n, g)][:].rearrange("p c j -> p (c j)"),
            )
            w_codes[(n, g)] = (codes, scales)

        def multiply(n, g, t):
            codes, scales = w_codes[(n, g)]
            if g == 0:
                acc[(n, t)] = acc_psum.tile([P, BANK], F32, name="acc", tag="bank")
            nc.tensor.matmul_mx(
                out=acc[(n, t)][:],
                lhsT=x_codes[t][:, g * P : (g + 1) * P].bitcast(FP8X4),
                lhsT_scale=x_scales[t][:, g * P : (g + 1) * P],
                rhs=codes[:].bitcast(FP8X4),
                rhs_scale=scales[:],
                start=(g == 0),
                stop=(g == PASSES - 1),
            )

        q_tiles = {}
        products = {}

        def add_bias(n, t):
            if t == 0:
                q_tile = q_pool.tile([P, TOKEN_TILES, Q_WIDTH], F32, name="q_tile")
                q_tiles[n] = q_tile
            nc.vector.tensor_tensor(
                out=q_tiles[n][:, t, 0:BANK],
                in0=acc[(n, t)][:],
                in1=bias_sb[:, first_column(n) : first_column(n) + BANK],
                op=ADD,
            )

        def heads_of(n):
            first = (NOPE - first_column(n)) % HEAD
            return first, (BANK - first + NOPE) // HEAD

        def rotated_view(n, s):
            first, heads = heads_of(n)
            view = q_tiles[n][:, 2 * s : 2 * s + 2, first : first + heads * HEAD].rearrange(
                "p a (h d) -> p a h d", d=HEAD
            )
            return view[:, :, :, 0:ROPE].rearrange("p a h (j e) -> p a h j e", e=2)

        def rotated_both(n):
            first, heads = heads_of(n)
            view = q_tiles[n][:, :, first : first + heads * HEAD].rearrange(
                "p (s a) (h d) -> p s a h d", a=2, d=HEAD
            )
            return view[:, :, :, :, 0:ROPE].rearrange("p s a h (j e) -> p s a h j e", e=2)

        def product_tiles(n):
            heads = heads_of(n)[1]
            size = TOKEN_TILES * heads * ROPE
            pair = []
            for name in ("by_cos", "by_sin"):
                flat = product_pool.tile([P, TOKEN_TILES * MAX_HEADS * ROPE], F32, name=name)
                pair.append(
                    flat[:, 0:size].rearrange(
                        "p (s a h j e) -> p s a h j e", s=2, a=2, h=heads, e=2
                    )
                )
            products[n] = pair

        def rotation_products(n):
            product_tiles(n)
            heads = heads_of(n)[1]
            for product, table in zip(products[n], (cos_table, sin_table)):
                nc.vector.tensor_tensor(
                    out=product,
                    in0=rotated_both(n),
                    in1=table[:, :, 0:heads].unsqueeze(1).to_broadcast([P, 2, 2, heads, PAIRS, 2]),
                    op=MULT,
                )

        def rotation_sum(n, engine=nc.vector):
            by_cos, by_sin = products[n]
            engine.tensor_tensor(
                out=rotated_both(n),
                in0=by_cos,
                in1=by_sin[:, :, :, :, :, ::-1],
                op=ADD,
            )

        def batch_product(n, s, i):
            heads = heads_of(n)[1]
            nc.vector.tensor_tensor(
                out=products[n][i][:, s],
                in0=rotated_view(n, s),
                in1=(cos_table, sin_table)[i][:, :, 0:heads],
                op=MULT,
            )

        def batch_sum(n, s):
            by_cos, by_sin = products[n]
            nc.vector.tensor_tensor(
                out=rotated_view(n, s),
                in0=by_cos[:, s],
                in1=by_sin[:, s, :, :, :, ::-1],
                op=ADD,
            )

        def tile_sum(n, t):
            s, a = divmod(t, 2)
            by_cos, by_sin = products[n]
            nc.vector.tensor_tensor(
                out=rotated_view(n, s)[:, a],
                in0=by_cos[:, s, a],
                in1=by_sin[:, s, a, :, :, ::-1],
                op=ADD,
            )

        def store(n, first_tile, tiles):
            rows = slice(first_tile * P, (first_tile + tiles) * P)
            nc.sync.dma_start(
                out=out_rows[rows, first_column(n) : first_column(n) + BANK].rearrange(
                    "(t p) c -> p t c", p=P
                ),
                in_=q_tiles[n][:, first_tile : first_tile + tiles, 0:BANK],
            )

        cos_table = const.tile([P, 2, MAX_HEADS, PAIRS, 2], BF16, name="cos_table")
        sin_table = const.tile([P, 2, MAX_HEADS, PAIRS, 2], BF16, name="sin_table")
        nc.vector.tensor_copy(
            out=cos_table[:],
            in_=cos_sb[:].unsqueeze(2).unsqueeze(4).to_broadcast([P, 2, MAX_HEADS, PAIRS, 2]),
        )
        sin_heads = sin_sb[:].unsqueeze(2).to_broadcast([P, 2, MAX_HEADS, PAIRS])
        nc.vector.tensor_copy(out=sin_table[:, :, :, :, 0], in_=sin_heads)
        nc.vector.tensor_scalar_mul(out=sin_table[:, :, :, :, 1], in0=sin_heads, scalar1=-1.0)

        def prepare(n, g):
            regroup_gpsimd(n, g)
            regroup(n, g)

        def multiply_some(n, passes, tiles):
            for t in tiles:
                for g in passes:
                    multiply(n, g, t)

        order = [(n, g) for n in range(2, PANELS) for g in range(PASSES)]
        SCALAR_AHEAD = 3

        def ahead(k):
            if k < len(order):
                prepare(order[k][0], order[k][1])

        prepare(0, 0)
        x_flip(0)
        quantise(0, 0)
        prepare(1, 0)
        x_quantise(0)
        spread_bias(0)
        prepare(0, 1)
        quantise(1, 0)
        quantise(0, 1)
        x_flip(1)
        prepare(1, 1)
        spread_bias(1)
        multiply_some(0, (0, 1), (0,))
        x_quantise(1)
        prepare(0, 2)
        quantise(1, 1)
        quantise(0, 2)
        x_flip(2)
        prepare(1, 2)
        spread_bias(2)
        multiply_some(0, (0, 1), (1,))
        multiply_some(0, (2,), (0, 1))
        x_quantise(2)
        prepare(0, 3)
        quantise(1, 2)
        quantise(0, 3)
        x_flip(3)
        prepare(1, 3)
        multiply_some(0, (0, 1, 2), (2,))
        multiply_some(0, (3,), (0, 1, 2))
        x_quantise(3)
        multiply_some(0, range(PASSES), (3,))
        for k in range(SCALAR_AHEAD):
            ahead(k)
        for t in range(TOKEN_TILES):
            add_bias(0, t)
        quantise(1, 3)
        multiply_some(1, range(PASSES), range(TOKEN_TILES))
        rotation_products(0)

        last = LAST
        for k, (n, g) in enumerate(order):
            ahead(k + SCALAR_AHEAD)
            quantise(n, g)
            if n == 2:
                if g == 0:
                    rotation_sum(0)
                    store(0, 0, TOKEN_TILES)
                if g == 1:
                    for t in range(TOKEN_TILES):
                        add_bias(1, t)
                    rotation_products(1)
            else:
                if g == 0:
                    if n == last:
                        rotation_products(n - 2)
                        rotation_sum(n - 2, nc.gpsimd)
                        store(n - 2, 0, TOKEN_TILES)
                    for t in range(TOKEN_TILES):
                        add_bias(n - 1, t)
                if g == 1 and n != last - 1:
                    rotation_products(n - 1)
            if g == 3 and n != last - 1:
                rotation_sum(n - 1)
                store(n - 1, 0, TOKEN_TILES)
            for t in range(TOKEN_TILES):
                multiply(n, g, t)

        product_tiles(last)
        add_bias(last, 0)
        add_bias(last, 1)
        batch_product(last, 0, 0)
        batch_product(last, 0, 1)
        add_bias(last, 2)
        add_bias(last, 3)
        batch_sum(last, 0)
        store(last, 0, 2)
        batch_product(last, 1, 0)
        batch_product(last, 1, 1)
        for t in (2, 3):
            tile_sum(last, t)
            store(last, t, 1)
